import numpy as np
import ml_dtypes


def mxq(x, axis, fmt="e4m3"):
    dtype, down = {"e4m3": (ml_dtypes.float8_e4m3fn, 7), "e5m2": (ml_dtypes.float8_e5m2, 14)}[fmt]
    v = np.moveaxis(np.asarray(x, np.float32).astype(ml_dtypes.bfloat16).astype(np.float64), axis, -1)
    blocks = v.reshape(v.shape[:-1] + (-1, 32))
    amax = np.abs(blocks).max(-1, keepdims=True)
    byte = np.maximum(np.where(amax > 0, np.frexp(amax)[1] - 1 + 127, 0) - down, 1)
    scale = np.exp2(byte - 127.0)
    codes = (blocks / scale).astype(np.float32).astype(dtype).astype(np.float64)
    return np.moveaxis((codes * scale).reshape(v.shape), -1, axis)


WIDE = False


def mx_kscale(k):
    if not WIDE:
        return np.ones(k)
    levels = np.array([20, -20, 10, -10, 0])
    a = np.random.permutation(np.resize(levels, k // 512 * 4)).reshape(k // 512, 4)
    idx = np.arange(k)
    return np.exp2(a[idx // 512, idx % 128 // 32])


BF16 = ml_dtypes.bfloat16


def bf(x):
    return np.asarray(x, np.float32).astype(BF16)


def f64(x):
    return np.asarray(x).astype(np.float64)


B, S, IN, OUT, GROUP = 4, 1024, 1024, 1024, 128
SCALE_RATIO = 1.4171
EPS = 1e-6


def softplus(v):
    return np.logaddexp(v, 0.0)


def inv_softplus(b):
    return np.where(b > 30.0, b, np.log(np.expm1(np.minimum(b, 30.0)) + EPS))


def build_w(weight_logits, raw_scales):
    wl = f64(weight_logits)
    rows, cols = wl.shape
    q = np.where(wl.reshape(rows, cols // GROUP, GROUP) >= 0, 1.0, -1.0)
    scales = softplus(f64(raw_scales)) + EPS
    return (q * scales[:, :, None]).reshape(rows, cols)


def setup_inputs():
    u = mx_kscale(OUT)
    t = u / u.max()
    x = np.random.standard_normal((B, S, IN))
    latent = np.random.standard_normal((OUT, IN)) / np.sqrt(IN)
    base_scale = np.abs(latent.reshape(OUT, IN // GROUP, GROUP)).mean(axis=-1) * SCALE_RATIO
    base_scale = base_scale * np.exp2(np.random.uniform(-1.0, 1.0, (OUT, IN // GROUP)))
    raw_scales = inv_softplus(base_scale / t[:, None])
    g = np.random.standard_normal((B, S, OUT)) * np.exp2(np.random.randint(-12, 1, (B, S, 1))) * 8.0 * t
    return {"x": bf(x), "weight_logits": bf(latent), "raw_scales": bf(raw_scales), "grad_out": bf(g)}


def reference(x, weight_logits, raw_scales, grad_out):
    w = build_w(weight_logits, raw_scales)
    return mxq(f64(grad_out), 2, "e5m2") @ mxq(w, 0, "e4m3")

@@ -1,0 +1,215 @@
+from contextlib import ExitStack
+
+import concourse.mybir as mybir
+from concourse.masks import make_identity
+
+F32 = mybir.dt.float32
+BF16 = mybir.dt.bfloat16
+U32 = mybir.dt.uint32
+U8 = mybir.dt.uint8
+E4M3X4 = mybir.dt.float8_e4m3fn_x4
+E5M2X4 = mybir.dt.float8_e5m2_x4
+ALU = mybir.AluOpType
+ACT = mybir.ActivationFunctionType
+
+P = 128
+PACK = 4
+K_PASS = P * PACK
+
+TOKENS = 4 * 1024
+OUT_F = 1024
+IN_F = 1024
+GROUP = 128
+GROUPS = IN_F // GROUP
+EPS = 1e-6
+
+PASSES = OUT_F // K_PASS
+N_MOVE = 512
+HALVES = IN_F // N_MOVE
+GROUPS_PER_HALF = N_MOVE // GROUP
+
+TILES = 4
+CHUNK_TOKENS = TILES * P
+CHUNKS = TOKENS // CHUNK_TOKENS
+STORE_TILES = 2
+
+FIRST_CHUNKS = 2
+AHEAD = 2
+
+FLOPS = 2 * TOKENS * OUT_F * IN_F
+BYTES = 2 * TOKENS * OUT_F + 2 * OUT_F * IN_F + 2 * OUT_F * GROUPS + 4 * TOKENS * IN_F
+
+
+def tile_groupedstelinear_t_kernel(tc, x, weight_logits, raw_scales, grad_out, out):
+    nc = tc.nc
+    grad_rows = grad_out.flatten_outer_dims()
+    out_rows = out.flatten_outer_dims()
+
+    with ExitStack() as ctx:
+        consts = ctx.enter_context(tc.tile_pool(name="consts", bufs=1))
+        weights = ctx.enter_context(tc.tile_pool(name="weights", bufs=1))
+        grad_pool = ctx.enter_context(tc.tile_pool(name="grad", bufs=CHUNKS))
+        grouped_pool = ctx.enter_context(tc.tile_pool(name="grouped", bufs=4))
+        codes_pool = ctx.enter_context(tc.tile_pool(name="codes", bufs=FIRST_CHUNKS + AHEAD))
+        staged_pool = ctx.enter_context(tc.tile_pool(name="staged", bufs=4))
+        flipped_pool = ctx.enter_context(tc.psum_pool(name="flipped", bufs=4))
+        acc_pool = ctx.enter_context(tc.psum_pool(name="acc", bufs=4))
+
+        raw = consts.tile([P, PASSES, PACK, GROUPS], BF16)
+        nc.sync.dma_start(
+            out=raw[:].rearrange("p c (u e) g -> p (c u) (e g)", e=2),
+            in_=raw_scales.rearrange("(cu p e) g -> p cu (e g)", p=P, e=2),
+        )
+        logits = weights.tile([P, PASSES, PACK, IN_F], BF16)
+        for c in range(PASSES):
+            nc.sync.dma_start(
+                out=logits[:, c, :, :].rearrange("p (u e) i -> p u (e i)", e=2),
+                in_=weight_logits[c * K_PASS : (c + 1) * K_PASS, :].rearrange("(u p e) i -> p u (e i)", p=P, e=2),
+            )
+        grad_chunks = []
+        for chunk in range(CHUNKS):
+            grad = grad_pool.tile([P, TILES, OUT_F], BF16)
+            nc.sync.dma_start(
+                out=grad[:],
+                in_=grad_rows[chunk * CHUNK_TOKENS : (chunk + 1) * CHUNK_TOKENS, :].rearrange(
+                    "(p j) o -> p j o", j=TILES
+                ),
+            )
+            grad_chunks.append(grad)
+
+        identity = consts.tile([P, P], F32)
+        make_identity(nc, identity[:])
+
+        minus_abs = consts.tile([P, PASSES, PACK, GROUPS], F32)
+        nc.vector.scalar_tensor_tensor(
+            out=minus_abs[:], in0=raw[:], scalar=-1.0, in1=raw[:], op0=ALU.mult, op1=ALU.min
+        )
+        decay = consts.tile([P, PASSES, PACK, GROUPS], F32)
+        nc.scalar.activation(out=decay[:], in_=minus_abs[:], func=ACT.Exp)
+        log_term = consts.tile([P, PASSES, PACK, GROUPS], F32)
+        nc.scalar.activation(out=log_term[:], in_=decay[:], func=ACT.Ln, bias=1.0)
+        softplus = consts.tile([P, PASSES, PACK, GROUPS], F32)
+        nc.vector.scalar_tensor_tensor(
+            out=softplus[:], in0=raw[:], scalar=0.0, in1=log_term[:], op0=ALU.max, op1=ALU.add
+        )
+        twice_scale = consts.tile([P, PASSES, PACK, GROUPS], F32)
+        nc.vector.tensor_scalar(
+            out=twice_scale[:], in0=softplus[:], scalar1=EPS, scalar2=2.0, op0=ALU.add, op1=ALU.mult
+        )
+
+        half_sign = weights.tile([P, PASSES, PACK, IN_F], BF16)
+        w_grouped = [
+            weights.tile([P, PASSES, N_MOVE, PACK], BF16, align_bytes=64, name="w_grouped%d" % half)
+            for half in range(HALVES)
+        ]
+        w_codes = [
+            weights.tile([P, PASSES, N_MOVE], U32, align_bytes=64, name="w_codes%d" % half)
+            for half in range(HALVES)
+        ]
+        w_scales = [
+            weights.tile([P, PASSES, N_MOVE], U8, align_bytes=64, name="w_scales%d" % half)
+            for half in range(HALVES)
+        ]
+
+        def build_w(half):
+            cols = slice(half * N_MOVE, (half + 1) * N_MOVE)
+            groups = slice(half * GROUPS_PER_HALF, (half + 1) * GROUPS_PER_HALF)
+            for c in range(PASSES):
+                nc.vector.tensor_scalar(
+                    out=half_sign[:, c, :, cols],
+                    in0=logits[:, c, :, cols],
+                    scalar1=0.0,
+                    scalar2=0.5,
+                    op0=ALU.is_ge,
+                    op1=ALU.subtract,
+                )
+            for c in range(PASSES):
+                nc.vector.tensor_tensor(
+                    out=w_grouped[half][:, c, :, :].rearrange("p (g i) t -> p g i t", i=GROUP),
+                    in0=half_sign[:, c, :, cols].rearrange("p t (g i) -> p g i t", i=GROUP),
+                    in1=twice_scale[:, c, :, groups]
+                    .rearrange("p t g -> p g t")
+                    .unsqueeze(2)
+                    .to_broadcast([P, GROUPS_PER_HALF, GROUP, PACK]),
+                    op=ALU.mult,
+                )
+            nc.vector.quantize_mx(
+                out=w_codes[half][:].rearrange("p c n -> p (c n)").bitcast(E4M3X4),
+                scales=w_scales[half][:].rearrange("p c n -> p (c n)"),
+                in_=w_grouped[half][:].rearrange("p c n t -> p (c n t)"),
+            )
+
+        grad_codes = {}
+        grad_scales = {}
+
+        def prepare(chunk):
+            codes = codes_pool.tile([P, TILES, PASSES, P], U32, align_bytes=64)
+            scales = codes_pool.tile([P, TILES, PASSES, P], U8, align_bytes=64)
+            grad_codes[chunk] = codes
+            grad_scales[chunk] = scales
+            for j in range(TILES):
+                words = grad_chunks[chunk][:, j, :].bitcast(F32)
+                flipped = flipped_pool.tile([P, PASSES * 2, P], F32)
+                for cu in range(PASSES * 2):
+                    nc.tensor.transpose(flipped[:, cu, :], words[:, cu * P : (cu + 1) * P], identity[:])
+                grouped = grouped_pool.tile([P, PASSES * P * PACK], BF16, align_bytes=64)
+                nc.scalar.copy(
+                    out=grouped[:].bitcast(F32).rearrange("p (c r u) -> p c r u", c=PASSES, u=2),
+                    in_=flipped[:].rearrange("p (c u) r -> p c r u", u=2),
+                )
+                nc.vector.quantize_mx(
+                    out=codes[:, j, :, :].rearrange("p c r -> p (c r)").bitcast(E5M2X4),
+                    scales=scales[:, j, :, :].rearrange("p c r -> p (c r)"),
+                    in_=grouped[:],
+                )
+
+        staged_chunks = {}
+
+        def multiply(chunk, j, half):
+            acc = acc_pool.tile([P, N_MOVE], F32)
+            for c in range(PASSES):
+                nc.tensor.matmul_mx(
+                    out=acc[:],
+                    lhsT=grad_codes[chunk][:, j, c, :].bitcast(E5M2X4),
+                    lhsT_scale=grad_scales[chunk][:, j, c, :],
+                    rhs=w_codes[half][:, c, :].bitcast(E4M3X4),
+                    rhs_scale=w_scales[half][:, c, :],
+                    start=(c == 0),
+                    stop=(c == PASSES - 1),
+                )
+            target = staged_chunks[chunk][:, j, half * N_MOVE : (half + 1) * N_MOVE]
+            if half == 0:
+                nc.scalar.copy(out=target, in_=acc[:])
+            else:
+                nc.vector.tensor_copy(out=target, in_=acc[:])
+
+        def store(chunk, first_tile):
+            tiles = slice(first_tile, first_tile + STORE_TILES)
+            nc.sync.dma_start(
+                out=out_rows[chunk * CHUNK_TOKENS : (chunk + 1) * CHUNK_TOKENS, :].rearrange(
+                    "(p j) i -> p j i", j=TILES
+                )[:, tiles, :],
+                in_=staged_chunks[chunk][:, tiles, :],
+            )
+
+        build_w(0)
+        for chunk in range(AHEAD):
+            prepare(chunk)
+        build_w(1)
+
+        sweeps = (
+            [(chunk, (0,)) for chunk in range(FIRST_CHUNKS)]
+            + [(chunk, (1,)) for chunk in range(FIRST_CHUNKS)]
+            + [(chunk, (0, 1)) for chunk in range(FIRST_CHUNKS, CHUNKS)]
+        )
+        for chunk, halves in sweeps:
+            if 0 in halves:
+                staged = staged_pool.tile([P, TILES, IN_F], F32)
+                staged_chunks[chunk] = staged
+            for j in range(TILES):
+                for half in halves:
+                    multiply(chunk, j, half)
+                if 1 in halves and (j + 1) % STORE_TILES == 0:
+                    store(chunk, j + 1 - STORE_TILES)
+            if 0 in halves and chunk + AHEAD < CHUNKS:
+                prepare(chunk + AHEAD)

@@ -34,7 +34,6 @@ CHUNKS = TOKENS // CHUNK_TOKENS
 STORE_TILES = 2
 
 FIRST_CHUNKS = 2
-AHEAD = 2
 
 FLOPS = 2 * TOKENS * OUT_F * IN_F
 BYTES = 2 * TOKENS * OUT_F + 2 * OUT_F * IN_F + 2 * OUT_F * GROUPS + 4 * TOKENS * IN_F
@@ -46,11 +45,12 @@ def tile_groupedstelinear_t_kernel(tc, x, weight_logits, raw_scales, grad_out, o
     out_rows = out.flatten_outer_dims()
 
     with ExitStack() as ctx:
+        ctx.enter_context(tc.manual_schedule())
         consts = ctx.enter_context(tc.tile_pool(name="consts", bufs=1))
         weights = ctx.enter_context(tc.tile_pool(name="weights", bufs=1))
         grad_pool = ctx.enter_context(tc.tile_pool(name="grad", bufs=CHUNKS))
         grouped_pool = ctx.enter_context(tc.tile_pool(name="grouped", bufs=4))
-        codes_pool = ctx.enter_context(tc.tile_pool(name="codes", bufs=FIRST_CHUNKS + AHEAD))
+        codes_pool = ctx.enter_context(tc.tile_pool(name="codes", bufs=TILES * (FIRST_CHUNKS + 1)))
         staged_pool = ctx.enter_context(tc.tile_pool(name="staged", bufs=4))
         flipped_pool = ctx.enter_context(tc.psum_pool(name="flipped", bufs=4))
         acc_pool = ctx.enter_context(tc.psum_pool(name="acc", bufs=4))
@@ -61,13 +61,22 @@ def tile_groupedstelinear_t_kernel(tc, x, weight_logits, raw_scales, grad_out, o
             in_=raw_scales.rearrange("(cu p e) g -> p cu (e g)", p=P, e=2),
         )
         logits = weights.tile([P, PASSES, PACK, IN_F], BF16)
-        for c in range(PASSES):
-            nc.sync.dma_start(
-                out=logits[:, c, :, :].rearrange("p (u e) i -> p u (e i)", e=2),
-                in_=weight_logits[c * K_PASS : (c + 1) * K_PASS, :].rearrange("(u p e) i -> p u (e i)", p=P, e=2),
-            )
+
+        def load_logits(half):
+            cols = slice(half * N_MOVE, (half + 1) * N_MOVE)
+            for c in range(PASSES):
+                for u in range(2):
+                    first = c * K_PASS + u * 2 * P
+                    nc.sync.dma_start(
+                        out=logits[:, c, 2 * u : 2 * u + 2, cols],
+                        in_=weight_logits[first : first + 2 * P, cols].rearrange("(p e) i -> p e i", e=2),
+                    )
+
+        load_logits(0)
         grad_chunks = []
         for chunk in range(CHUNKS):
+            if chunk == 1:
+                load_logits(1)
             grad = grad_pool.tile([P, TILES, OUT_F], BF16)
             nc.sync.dma_start(
                 out=grad[:],
@@ -88,16 +97,11 @@ def tile_groupedstelinear_t_kernel(tc, x, weight_logits, raw_scales, grad_out, o
         nc.scalar.activation(out=decay[:], in_=minus_abs[:], func=ACT.Exp)
         log_term = consts.tile([P, PASSES, PACK, GROUPS], F32)
         nc.scalar.activation(out=log_term[:], in_=decay[:], func=ACT.Ln, bias=1.0)
-        softplus = consts.tile([P, PASSES, PACK, GROUPS], F32)
-        nc.vector.scalar_tensor_tensor(
-            out=softplus[:], in0=raw[:], scalar=0.0, in1=log_term[:], op0=ALU.max, op1=ALU.add
-        )
-        twice_scale = consts.tile([P, PASSES, PACK, GROUPS], F32)
-        nc.vector.tensor_scalar(
-            out=twice_scale[:], in0=softplus[:], scalar1=EPS, scalar2=2.0, op0=ALU.add, op1=ALU.mult
-        )
 
-        half_sign = weights.tile([P, PASSES, PACK, IN_F], BF16)
+        half_sign = [
+            weights.tile([P, PASSES, N_MOVE, PACK], BF16, align_bytes=64, name="half_sign%d" % half)
+            for half in range(HALVES)
+        ]
         w_grouped = [
             weights.tile([P, PASSES, N_MOVE, PACK], BF16, align_bytes=64, name="w_grouped%d" % half)
             for half in range(HALVES)
@@ -111,77 +115,82 @@ def tile_groupedstelinear_t_kernel(tc, x, weight_logits, raw_scales, grad_out, o
             for half in range(HALVES)
         ]
 
-        def build_w(half):
+        def make_signs(half, c):
             cols = slice(half * N_MOVE, (half + 1) * N_MOVE)
-            groups = slice(half * GROUPS_PER_HALF, (half + 1) * GROUPS_PER_HALF)
-            for c in range(PASSES):
-                nc.vector.tensor_scalar(
-                    out=half_sign[:, c, :, cols],
-                    in0=logits[:, c, :, cols],
-                    scalar1=0.0,
-                    scalar2=0.5,
-                    op0=ALU.is_ge,
-                    op1=ALU.subtract,
-                )
-            for c in range(PASSES):
-                nc.vector.tensor_tensor(
-                    out=w_grouped[half][:, c, :, :].rearrange("p (g i) t -> p g i t", i=GROUP),
-                    in0=half_sign[:, c, :, cols].rearrange("p t (g i) -> p g i t", i=GROUP),
-                    in1=twice_scale[:, c, :, groups]
-                    .rearrange("p t g -> p g t")
-                    .unsqueeze(2)
-                    .to_broadcast([P, GROUPS_PER_HALF, GROUP, PACK]),
-                    op=ALU.mult,
-                )
-            nc.vector.quantize_mx(
-                out=w_codes[half][:].rearrange("p c n -> p (c n)").bitcast(E4M3X4),
-                scales=w_scales[half][:].rearrange("p c n -> p (c n)"),
-                in_=w_grouped[half][:].rearrange("p c n t -> p (c n t)"),
+            nc.vector.tensor_scalar(
+                out=half_sign[half][:, c, :, :],
+                in0=logits[:, c, :, cols].rearrange("p t i -> p i t"),
+                scalar1=0.0,
+                scalar2=0.5,
+                op0=ALU.is_ge,
+                op1=ALU.subtract,
             )
 
+        def make_w(half, c):
+            groups = slice(half * GROUPS_PER_HALF, (half + 1) * GROUPS_PER_HALF)
+            nc.vector.tensor_tensor(
+                out=w_grouped[half][:, c, :, :].rearrange("p (g i) t -> p g i t", i=GROUP),
+                in0=half_sign[half][:, c, :, :].rearrange("p (g i) t -> p g i t", i=GROUP),
+                in1=twice_scale[:, c, groups, :].unsqueeze(2).to_broadcast([P, GROUPS_PER_HALF, GROUP, PACK]),
+                op=ALU.mult,
+            )
+
+        def quantize_w(half, c):
+            nc.vector.quantize_mx(
+                out=w_codes[half][:, c, :].bitcast(E4M3X4),
+                scales=w_scales[half][:, c, :],
+                in_=w_grouped[half][:, c, :, :].rearrange("p n t -> p (n t)"),
+            )
+
+        flipped_tiles = {}
+        grouped_tiles = {}
         grad_codes = {}
         grad_scales = {}
 
-        def prepare(chunk):
-            codes = codes_pool.tile([P, TILES, PASSES, P], U32, align_bytes=64)
-            scales = codes_pool.tile([P, TILES, PASSES, P], U8, align_bytes=64)
-            grad_codes[chunk] = codes
-            grad_scales[chunk] = scales
-            for j in range(TILES):
-                words = grad_chunks[chunk][:, j, :].bitcast(F32)
-                flipped = flipped_pool.tile([P, PASSES * 2, P], F32)
-                for cu in range(PASSES * 2):
-                    nc.tensor.transpose(flipped[:, cu, :], words[:, cu * P : (cu + 1) * P], identity[:])
-                grouped = grouped_pool.tile([P, PASSES * P * PACK], BF16, align_bytes=64)
-                nc.scalar.copy(
-                    out=grouped[:].bitcast(F32).rearrange("p (c r u) -> p c r u", c=PASSES, u=2),
-                    in_=flipped[:].rearrange("p (c u) r -> p c r u", u=2),
-                )
-                nc.vector.quantize_mx(
-                    out=codes[:, j, :, :].rearrange("p c r -> p (c r)").bitcast(E5M2X4),
-                    scales=scales[:, j, :, :].rearrange("p c r -> p (c r)"),
-                    in_=grouped[:],
-                )
+        def flip(chunk, j):
+            words = grad_chunks[chunk][:, j, :].bitcast(F32)
+            flipped = flipped_pool.tile([P, PASSES * 2, P], F32)
+            flipped_tiles[chunk, j] = flipped
+            for cu in range(PASSES * 2):
+                nc.tensor.transpose(flipped[:, cu, :], words[:, cu * P : (cu + 1) * P], identity[:])
+
+        def group(chunk, j):
+            grouped = grouped_pool.tile([P, PASSES * P * PACK], BF16, align_bytes=64)
+            grouped_tiles[chunk, j] = grouped
+            nc.scalar.copy(
+                out=grouped[:].bitcast(F32).rearrange("p (c r u) -> p c r u", c=PASSES, u=2),
+                in_=flipped_tiles[chunk, j][:].rearrange("p (c u) r -> p c r u", u=2),
+            )
+
+        def quantize_grad(chunk, j):
+            codes = codes_pool.tile([P, PASSES, P], U32, align_bytes=64)
+            scales = codes_pool.tile([P, PASSES, P], U8, align_bytes=64)
+            grad_codes[chunk, j] = codes
+            grad_scales[chunk, j] = scales
+            nc.vector.quantize_mx(
+                out=codes[:].rearrange("p c r -> p (c r)").bitcast(E5M2X4),
+                scales=scales[:].rearrange("p c r -> p (c r)"),
+                in_=grouped_tiles[chunk, j][:],
+            )
 
         staged_chunks = {}
 
-        def multiply(chunk, j, half):
+        def multiply(chunk, j, half, copy_out):
             acc = acc_pool.tile([P, N_MOVE], F32)
             for c in range(PASSES):
                 nc.tensor.matmul_mx(
                     out=acc[:],
-                    lhsT=grad_codes[chunk][:, j, c, :].bitcast(E5M2X4),
-                    lhsT_scale=grad_scales[chunk][:, j, c, :],
+                    lhsT=grad_codes[chunk, j][:, c, :].bitcast(E5M2X4),
+                    lhsT_scale=grad_scales[chunk, j][:, c, :],
                     rhs=w_codes[half][:, c, :].bitcast(E4M3X4),
                     rhs_scale=w_scales[half][:, c, :],
                     start=(c == 0),
                     stop=(c == PASSES - 1),
                 )
-            target = staged_chunks[chunk][:, j, half * N_MOVE : (half + 1) * N_MOVE]
-            if half == 0:
-                nc.scalar.copy(out=target, in_=acc[:])
-            else:
-                nc.vector.tensor_copy(out=target, in_=acc[:])
+            if chunk not in staged_chunks:
+                staged = staged_pool.tile([P, TILES, IN_F], F32)
+                staged_chunks[chunk] = staged
+            copy_out(out=staged_chunks[chunk][:, j, half * N_MOVE : (half + 1) * N_MOVE], in_=acc[:])
 
         def store(chunk, first_tile):
             tiles = slice(first_tile, first_tile + STORE_TILES)
@@ -192,24 +201,73 @@ def tile_groupedstelinear_t_kernel(tc, x, weight_logits, raw_scales, grad_out, o
                 in_=staged_chunks[chunk][:, tiles, :],
             )
 
-        build_w(0)
-        for chunk in range(AHEAD):
-            prepare(chunk)
-        build_w(1)
+        def store_if_full(chunk, j):
+            if (j + 1) % STORE_TILES == 0:
+                store(chunk, j + 1 - STORE_TILES)
 
-        sweeps = (
-            [(chunk, (0,)) for chunk in range(FIRST_CHUNKS)]
-            + [(chunk, (1,)) for chunk in range(FIRST_CHUNKS)]
-            + [(chunk, (0, 1)) for chunk in range(FIRST_CHUNKS, CHUNKS)]
+        for c in range(PASSES):
+            make_signs(0, c)
+        softplus = consts.tile([P, PASSES, PACK, GROUPS], F32)
+        nc.vector.scalar_tensor_tensor(
+            out=softplus[:], in0=raw[:], scalar=0.0, in1=log_term[:], op0=ALU.max, op1=ALU.add
         )
-        for chunk, halves in sweeps:
-            if 0 in halves:
-                staged = staged_pool.tile([P, TILES, IN_F], F32)
-                staged_chunks[chunk] = staged
+        twice_scale = consts.tile([P, PASSES, GROUPS, PACK], BF16)
+        nc.vector.tensor_scalar(
+            out=twice_scale[:],
+            in0=softplus[:].rearrange("p c t g -> p c g t"),
+            scalar1=EPS,
+            scalar2=2.0,
+            op0=ALU.add,
+            op1=ALU.mult,
+        )
+        for j in range(TILES):
+            flip(0, j)
+            group(0, j)
+        for c in range(PASSES):
+            make_w(0, c)
+        quantize_w(0, 0)
+        quantize_grad(0, 0)
+        quantize_w(0, 1)
+        for j in range(1, TILES):
+            quantize_grad(0, j)
+
+        for c in range(PASSES):
+            make_signs(1, c)
+        for j in range(TILES):
+            multiply(0, j, 0, nc.scalar.copy)
+        for j in range(TILES):
+            flip(1, j)
+        for j in range(TILES):
+            group(1, j)
+            quantize_grad(1, j)
+        for c in range(PASSES):
+            make_w(1, c)
+        for c in range(PASSES):
+            quantize_w(1, c)
+        for j in range(TILES):
+            multiply(1, j, 0, nc.scalar.copy)
+
+        for j in range(TILES):
+            flip(2, j)
+        for chunk in range(FIRST_CHUNKS):
             for j in range(TILES):
-                for half in halves:
-                    multiply(chunk, j, half)
-                if 1 in halves and (j + 1) % STORE_TILES == 0:
-                    store(chunk, j + 1 - STORE_TILES)
-            if 0 in halves and chunk + AHEAD < CHUNKS:
-                prepare(chunk + AHEAD)
+                if j % 2 == 0:
+                    group(2, chunk * 2 + j // 2)
+                multiply(chunk, j, 1, nc.vector.tensor_copy if j % 2 == 0 else nc.scalar.copy)
+                if j % 2 == 0:
+                    quantize_grad(2, chunk * 2 + j // 2)
+                store_if_full(chunk, j)
+
+        for chunk in range(FIRST_CHUNKS, CHUNKS):
+            ahead = chunk + 1
+            if ahead < CHUNKS:
+                for j in range(TILES):
+                    flip(ahead, j)
+            for j in range(TILES):
+                if ahead < CHUNKS:
+                    group(ahead, j)
+                multiply(chunk, j, 0, nc.scalar.copy)
+                multiply(chunk, j, 1, nc.vector.tensor_copy)
+                if ahead < CHUNKS:
+                    quantize_grad(ahead, j)
+                store_if_full(chunk, j)

@@ -33,7 +33,8 @@ CHUNK_TOKENS = TILES * P
 CHUNKS = TOKENS // CHUNK_TOKENS
 STORE_TILES = 2
 
-FIRST_CHUNKS = 2
+FIRST_CHUNKS = 3
+HEAD_CHUNKS = 2
 
 FLOPS = 2 * TOKENS * OUT_F * IN_F
 BYTES = 2 * TOKENS * OUT_F + 2 * OUT_F * IN_F + 2 * OUT_F * GROUPS + 4 * TOKENS * IN_F
@@ -49,7 +50,7 @@ def tile_groupedstelinear_t_kernel(tc, x, weight_logits, raw_scales, grad_out, o
         consts = ctx.enter_context(tc.tile_pool(name="consts", bufs=1))
         weights = ctx.enter_context(tc.tile_pool(name="weights", bufs=1))
         grad_pool = ctx.enter_context(tc.tile_pool(name="grad", bufs=CHUNKS))
-        grouped_pool = ctx.enter_context(tc.tile_pool(name="grouped", bufs=4))
+        grouped_pool = ctx.enter_context(tc.tile_pool(name="grouped", bufs=HEAD_CHUNKS * TILES))
         codes_pool = ctx.enter_context(tc.tile_pool(name="codes", bufs=TILES * (FIRST_CHUNKS + 1)))
         staged_pool = ctx.enter_context(tc.tile_pool(name="staged", bufs=4))
         flipped_pool = ctx.enter_context(tc.psum_pool(name="flipped", bufs=4))
@@ -62,32 +63,49 @@ def tile_groupedstelinear_t_kernel(tc, x, weight_logits, raw_scales, grad_out, o
         )
         logits = weights.tile([P, PASSES, PACK, IN_F], BF16)
 
-        def load_logits(half):
+        def load_logits(half, c):
             cols = slice(half * N_MOVE, (half + 1) * N_MOVE)
-            for c in range(PASSES):
-                for u in range(2):
-                    first = c * K_PASS + u * 2 * P
-                    nc.sync.dma_start(
-                        out=logits[:, c, 2 * u : 2 * u + 2, cols],
-                        in_=weight_logits[first : first + 2 * P, cols].rearrange("(p e) i -> p e i", e=2),
-                    )
+            for u in range(2):
+                first = c * K_PASS + u * 2 * P
+                nc.sync.dma_start(
+                    out=logits[:, c, 2 * u : 2 * u + 2, cols],
+                    in_=weight_logits[first : first + 2 * P, cols].rearrange("(p e) i -> p e i", e=2),
+                )
 
-        load_logits(0)
         grad_chunks = []
-        for chunk in range(CHUNKS):
-            if chunk == 1:
-                load_logits(1)
-            grad = grad_pool.tile([P, TILES, OUT_F], BF16)
+
+        def load_grad(chunk, first_tile, count):
+            if first_tile == 0:
+                grad = grad_pool.tile([P, TILES, OUT_F], BF16)
+                grad_chunks.append(grad)
+            tiles = slice(first_tile, first_tile + count)
             nc.sync.dma_start(
-                out=grad[:],
+                out=grad_chunks[chunk][:, tiles, :],
                 in_=grad_rows[chunk * CHUNK_TOKENS : (chunk + 1) * CHUNK_TOKENS, :].rearrange(
                     "(p j) o -> p j o", j=TILES
-                ),
+                )[:, tiles, :],
             )
-            grad_chunks.append(grad)
+
+        load_logits(0, 0)
+        load_grad(0, 0, TILES // 2)
+        load_grad(0, TILES // 2, TILES // 2)
+        load_logits(0, 1)
+        load_grad(1, 0, TILES // 2)
+        load_grad(1, TILES // 2, TILES // 2)
+        for c in range(PASSES):
+            load_logits(1, c)
+        for chunk in range(HEAD_CHUNKS, CHUNKS):
+            load_grad(chunk, 0, TILES)
 
         identity = consts.tile([P, P], F32)
         make_identity(nc, identity[:])
+        zeros = consts.tile([P, N_MOVE], BF16)
+        nc.vector.memset(zeros[:], 0.0)
+
+        def keep_tensor_busy(count):
+            idle = acc_pool.tile([P, N_MOVE], F32, name="acc")
+            for step in range(count):
+                nc.tensor.matmul(idle[:], lhsT=zeros[:, :P], rhs=zeros[:], start=True, stop=True)
 
         minus_abs = consts.tile([P, PASSES, PACK, GROUPS], F32)
         nc.vector.scalar_tensor_tensor(
@@ -192,8 +210,8 @@ def tile_groupedstelinear_t_kernel(tc, x, weight_logits, raw_scales, grad_out, o
                 staged_chunks[chunk] = staged
             copy_out(out=staged_chunks[chunk][:, j, half * N_MOVE : (half + 1) * N_MOVE], in_=acc[:])
 
-        def store(chunk, first_tile):
-            tiles = slice(first_tile, first_tile + STORE_TILES)
+        def store(chunk, first_tile, count):
+            tiles = slice(first_tile, first_tile + count)
             nc.sync.dma_start(
                 out=out_rows[chunk * CHUNK_TOKENS : (chunk + 1) * CHUNK_TOKENS, :].rearrange(
                     "(p j) i -> p j i", j=TILES
@@ -202,11 +220,13 @@ def tile_groupedstelinear_t_kernel(tc, x, weight_logits, raw_scales, grad_out, o
             )
 
         def store_if_full(chunk, j):
-            if (j + 1) % STORE_TILES == 0:
-                store(chunk, j + 1 - STORE_TILES)
+            if chunk >= CHUNKS - 2:
+                store(chunk, j, 1)
+            elif (j + 1) % STORE_TILES == 0:
+                store(chunk, j + 1 - STORE_TILES, STORE_TILES)
 
-        for c in range(PASSES):
-            make_signs(0, c)
+        keep_tensor_busy(8)
+        make_signs(0, 0)
         softplus = consts.tile([P, PASSES, PACK, GROUPS], F32)
         nc.vector.scalar_tensor_tensor(
             out=softplus[:], in0=raw[:], scalar=0.0, in1=log_term[:], op0=ALU.max, op1=ALU.add
@@ -220,42 +240,52 @@ def tile_groupedstelinear_t_kernel(tc, x, weight_logits, raw_scales, grad_out, o
             op0=ALU.add,
             op1=ALU.mult,
         )
-        for j in range(TILES):
-            flip(0, j)
-            group(0, j)
-        for c in range(PASSES):
-            make_w(0, c)
+        for chunk in range(HEAD_CHUNKS):
+            for j in range(TILES):
+                flip(chunk, j)
+                group(chunk, j)
+                if j % 2 == 1:
+                    keep_tensor_busy(2)
+        make_w(0, 0)
         quantize_w(0, 0)
+        make_signs(0, 1)
         quantize_grad(0, 0)
+        make_w(0, 1)
         quantize_w(0, 1)
         for j in range(1, TILES):
             quantize_grad(0, j)
+        for chunk in range(1, HEAD_CHUNKS):
+            for j in range(TILES):
+                quantize_grad(chunk, j)
 
+        for chunk in range(HEAD_CHUNKS):
+            for j in range(TILES):
+                multiply(chunk, j, 0, nc.scalar.copy)
         for c in range(PASSES):
             make_signs(1, c)
-        for j in range(TILES):
-            multiply(0, j, 0, nc.scalar.copy)
-        for j in range(TILES):
-            flip(1, j)
-        for j in range(TILES):
-            group(1, j)
-            quantize_grad(1, j)
-        for c in range(PASSES):
-            make_w(1, c)
+        make_w(1, 0)
+        for chunk in range(HEAD_CHUNKS, FIRST_CHUNKS):
+            for j in range(TILES):
+                flip(chunk, j)
+            for j in range(TILES):
+                group(chunk, j)
+                quantize_grad(chunk, j)
+            for j in range(TILES):
+                multiply(chunk, j, 0, nc.scalar.copy)
+        make_w(1, 1)
         for c in range(PASSES):
             quantize_w(1, c)
-        for j in range(TILES):
-            multiply(1, j, 0, nc.scalar.copy)
 
         for j in range(TILES):
-            flip(2, j)
+            flip(FIRST_CHUNKS, j)
         for chunk in range(FIRST_CHUNKS):
             for j in range(TILES):
-                if j % 2 == 0:
-                    group(2, chunk * 2 + j // 2)
-                multiply(chunk, j, 1, nc.vector.tensor_copy if j % 2 == 0 else nc.scalar.copy)
-                if j % 2 == 0:
-                    quantize_grad(2, chunk * 2 + j // 2)
+                ahead, due = divmod(chunk * TILES + j, FIRST_CHUNKS)
+                if due == 0:
+                    group(FIRST_CHUNKS, ahead)
+                multiply(chunk, j, 1, nc.vector.tensor_copy if (chunk * TILES + j) % 2 == 0 else nc.scalar.copy)
+                if due == FIRST_CHUNKS - 1:
+                    quantize_grad(FIRST_CHUNKS, ahead)
                 store_if_full(chunk, j)
 
         for chunk in range(FIRST_CHUNKS, CHUNKS):

@@ -117,19 +117,19 @@ def tile_groupedstelinear_t_kernel(tc, x, weight_logits, raw_scales, grad_out, o
         nc.scalar.activation(out=log_term[:], in_=decay[:], func=ACT.Ln, bias=1.0)
 
         half_sign = [
-            weights.tile([P, PASSES, N_MOVE, PACK], BF16, align_bytes=64, name="half_sign%d" % half)
+            weights.tile([P, PASSES, N_MOVE, PACK], BF16, align_bytes=256, name="half_sign%d" % half)
             for half in range(HALVES)
         ]
         w_grouped = [
-            weights.tile([P, PASSES, N_MOVE, PACK], BF16, align_bytes=64, name="w_grouped%d" % half)
+            weights.tile([P, PASSES, N_MOVE, PACK], BF16, align_bytes=256, name="w_grouped%d" % half)
             for half in range(HALVES)
         ]
         w_codes = [
-            weights.tile([P, PASSES, N_MOVE], U32, align_bytes=64, name="w_codes%d" % half)
+            weights.tile([P, PASSES, N_MOVE], U32, align_bytes=256, name="w_codes%d" % half)
             for half in range(HALVES)
         ]
         w_scales = [
-            weights.tile([P, PASSES, N_MOVE], U8, align_bytes=64, name="w_scales%d" % half)
+            weights.tile([P, PASSES, N_MOVE], U8, align_bytes=256, name="w_scales%d" % half)
             for half in range(HALVES)
         ]
 
@@ -173,7 +173,7 @@ def tile_groupedstelinear_t_kernel(tc, x, weight_logits, raw_scales, grad_out, o
                 nc.tensor.transpose(flipped[:, cu, :], words[:, cu * P : (cu + 1) * P], identity[:])
 
         def group(chunk, j):
-            grouped = grouped_pool.tile([P, PASSES * P * PACK], BF16, align_bytes=64)
+            grouped = grouped_pool.tile([P, PASSES * P * PACK], BF16, align_bytes=256)
             grouped_tiles[chunk, j] = grouped
             nc.scalar.copy(
                 out=grouped[:].bitcast(F32).rearrange("p (c r u) -> p c r u", c=PASSES, u=2),
@@ -181,8 +181,8 @@ def tile_groupedstelinear_t_kernel(tc, x, weight_logits, raw_scales, grad_out, o
             )
 
         def quantize_grad(chunk, j):
-            codes = codes_pool.tile([P, PASSES, P], U32, align_bytes=64)
-            scales = codes_pool.tile([P, PASSES, P], U8, align_bytes=64)
+            codes = codes_pool.tile([P, PASSES, P], U32, align_bytes=256)
+            scales = codes_pool.tile([P, PASSES, P], U8, align_bytes=256)
             grad_codes[chunk, j] = codes
             grad_scales[chunk, j] = scales
             nc.vector.quantize_mx(

@@ -61,14 +61,16 @@ def tile_groupedstelinear_t_kernel(tc, x, weight_logits, raw_scales, grad_out, o
             out=raw[:].rearrange("p c (u e) g -> p (c u) (e g)", e=2),
             in_=raw_scales.rearrange("(cu p e) g -> p cu (e g)", p=P, e=2),
         )
-        logits = weights.tile([P, PASSES, PACK, IN_F], BF16)
+        logits = {}
 
         def load_logits(half, c):
+            rows = weights.tile([P, PACK, N_MOVE], BF16, name="logits%d%d" % (half, c))
+            logits[half, c] = rows
             cols = slice(half * N_MOVE, (half + 1) * N_MOVE)
             for u in range(2):
                 first = c * K_PASS + u * 2 * P
                 nc.sync.dma_start(
-                    out=logits[:, c, 2 * u : 2 * u + 2, cols],
+                    out=rows[:, 2 * u : 2 * u + 2, :],
                     in_=weight_logits[first : first + 2 * P, cols].rearrange("(p e) i -> p e i", e=2),
                 )
 
@@ -86,10 +88,10 @@ def tile_groupedstelinear_t_kernel(tc, x, weight_logits, raw_scales, grad_out, o
                 )[:, tiles, :],
             )
 
-        load_logits(0, 0)
+        for c in range(PASSES):
+            load_logits(0, c)
         load_grad(0, 0, TILES // 2)
         load_grad(0, TILES // 2, TILES // 2)
-        load_logits(0, 1)
         load_grad(1, 0, TILES // 2)
         load_grad(1, TILES // 2, TILES // 2)
         for c in range(PASSES):
@@ -134,10 +136,9 @@ def tile_groupedstelinear_t_kernel(tc, x, weight_logits, raw_scales, grad_out, o
         ]
 
         def make_signs(half, c):
-            cols = slice(half * N_MOVE, (half + 1) * N_MOVE)
             nc.vector.tensor_scalar(
-                out=half_sign[half][:, c, :, :],
-                in0=logits[:, c, :, cols].rearrange("p t i -> p i t"),
+                out=half_sign[half][:, c, :, :].rearrange("p (n i) t -> p n t i", i=PACK),
+                in0=logits[half, c][:].rearrange("p t (n i) -> p n t i", i=PACK),
                 scalar1=0.0,
                 scalar2=0.5,
                 op0=ALU.is_ge,
@@ -226,7 +227,8 @@ def tile_groupedstelinear_t_kernel(tc, x, weight_logits, raw_scales, grad_out, o
                 store(chunk, j + 1 - STORE_TILES, STORE_TILES)
 
         keep_tensor_busy(8)
-        make_signs(0, 0)
+        for c in range(PASSES):
+            make_signs(0, c)
         softplus = consts.tile([P, PASSES, PACK, GROUPS], F32)
         nc.vector.scalar_tensor_tensor(
             out=softplus[:], in0=raw[:], scalar=0.0, in1=log_term[:], op0=ALU.max, op1=ALU.add
@@ -246,11 +248,10 @@ def tile_groupedstelinear_t_kernel(tc, x, weight_logits, raw_scales, grad_out, o
                 group(chunk, j)
                 if j % 2 == 1:
                     keep_tensor_busy(2)
-        make_w(0, 0)
+        for c in range(PASSES):
+            make_w(0, c)
         quantize_w(0, 0)
-        make_signs(0, 1)
         quantize_grad(0, 0)
-        make_w(0, 1)
         quantize_w(0, 1)
         for j in range(1, TILES):
             quantize_grad(0, j)

@@ -29,11 +29,12 @@ HALVES = IN_F // N_MOVE
 GROUPS_PER_HALF = N_MOVE // GROUP
 
 TILES = 4
-CHUNK_TOKENS = TILES * P
-CHUNKS = TOKENS // CHUNK_TOKENS
-STORE_TILES = 2
+CHUNKS = TOKENS // (TILES * P)
+PAIR_TILES = 2 * TILES
+PAIRS = CHUNKS // 2
 
 FIRST_CHUNKS = 3
+EARLY = 2
 HEAD_CHUNKS = 2
 
 FLOPS = 2 * TOKENS * OUT_F * IN_F
@@ -42,14 +43,14 @@ BYTES = 2 * TOKENS * OUT_F + 2 * OUT_F * IN_F + 2 * OUT_F * GROUPS + 4 * TOKENS 
 
 def tile_groupedstelinear_t_kernel(tc, x, weight_logits, raw_scales, grad_out, out):
     nc = tc.nc
-    grad_rows = grad_out.flatten_outer_dims()
-    out_rows = out.flatten_outer_dims()
+    grad_view = grad_out.flatten_outer_dims().rearrange("(b p j) o -> p b j o", p=P, j=PAIR_TILES)
+    out_view = out.flatten_outer_dims().rearrange("(b p j) i -> p b j i", p=P, j=PAIR_TILES)
 
     with ExitStack() as ctx:
         ctx.enter_context(tc.manual_schedule())
         consts = ctx.enter_context(tc.tile_pool(name="consts", bufs=1))
         weights = ctx.enter_context(tc.tile_pool(name="weights", bufs=1))
-        grad_pool = ctx.enter_context(tc.tile_pool(name="grad", bufs=CHUNKS))
+        grad_pool = ctx.enter_context(tc.tile_pool(name="grad", bufs=PAIRS))
         grouped_pool = ctx.enter_context(tc.tile_pool(name="grouped", bufs=HEAD_CHUNKS * TILES))
         codes_pool = ctx.enter_context(tc.tile_pool(name="codes", bufs=TILES * (FIRST_CHUNKS + 1)))
         staged_pool = ctx.enter_context(tc.tile_pool(name="staged", bufs=4))
@@ -57,7 +58,7 @@ def tile_groupedstelinear_t_kernel(tc, x, weight_logits, raw_scales, grad_out, o
         acc_pool = ctx.enter_context(tc.psum_pool(name="acc", bufs=4))
 
         raw = consts.tile([P, PASSES, PACK, GROUPS], BF16)
-        nc.sync.dma_start(
+        nc.scalar.dma_start(
             out=raw[:].rearrange("p c (u e) g -> p (c u) (e g)", e=2),
             in_=raw_scales.rearrange("(cu p e) g -> p cu (e g)", p=P, e=2),
         )
@@ -74,30 +75,23 @@ def tile_groupedstelinear_t_kernel(tc, x, weight_logits, raw_scales, grad_out, o
                     in_=weight_logits[first : first + 2 * P, cols].rearrange("(p e) i -> p e i", e=2),
                 )
 
-        grad_chunks = []
+        grad_pairs = []
 
-        def load_grad(chunk, first_tile, count):
-            if first_tile == 0:
-                grad = grad_pool.tile([P, TILES, OUT_F], BF16)
-                grad_chunks.append(grad)
-            tiles = slice(first_tile, first_tile + count)
-            nc.sync.dma_start(
-                out=grad_chunks[chunk][:, tiles, :],
-                in_=grad_rows[chunk * CHUNK_TOKENS : (chunk + 1) * CHUNK_TOKENS, :].rearrange(
-                    "(p j) o -> p j o", j=TILES
-                )[:, tiles, :],
-            )
+        def load_grad(pair, tiles_at_once):
+            grad = grad_pool.tile([P, PAIR_TILES, OUT_F], BF16)
+            grad_pairs.append(grad)
+            for first in range(0, PAIR_TILES, tiles_at_once):
+                tiles = slice(first, first + tiles_at_once)
+                nc.sync.dma_start(out=grad[:, tiles, :], in_=grad_view[:, pair, tiles, :])
 
         for c in range(PASSES):
             load_logits(0, c)
-        load_grad(0, 0, TILES // 2)
-        load_grad(0, TILES // 2, TILES // 2)
-        load_grad(1, 0, TILES // 2)
-        load_grad(1, TILES // 2, TILES // 2)
+        load_grad(0, 2)
         for c in range(PASSES):
             load_logits(1, c)
-        for chunk in range(HEAD_CHUNKS, CHUNKS):
-            load_grad(chunk, 0, TILES)
+        load_grad(1, TILES)
+        for pair in range(2, PAIRS):
+            load_grad(pair, PAIR_TILES)
 
         identity = consts.tile([P, P], F32)
         make_identity(nc, identity[:])
@@ -167,7 +161,7 @@ def tile_groupedstelinear_t_kernel(tc, x, weight_logits, raw_scales, grad_out, o
         grad_scales = {}
 
         def flip(chunk, j):
-            words = grad_chunks[chunk][:, j, :].bitcast(F32)
+            words = grad_pairs[chunk // 2][:, chunk % 2 * TILES + j, :].bitcast(F32)
             flipped = flipped_pool.tile([P, PASSES * 2, P], F32)
             flipped_tiles[chunk, j] = flipped
             for cu in range(PASSES * 2):
@@ -212,19 +206,21 @@ def tile_groupedstelinear_t_kernel(tc, x, weight_logits, raw_scales, grad_out, o
             copy_out(out=staged_chunks[chunk][:, j, half * N_MOVE : (half + 1) * N_MOVE], in_=acc[:])
 
         def store(chunk, first_tile, count):
-            tiles = slice(first_tile, first_tile + count)
+            offset = chunk % 2 * TILES + first_tile
             nc.sync.dma_start(
-                out=out_rows[chunk * CHUNK_TOKENS : (chunk + 1) * CHUNK_TOKENS, :].rearrange(
-                    "(p j) i -> p j i", j=TILES
-                )[:, tiles, :],
-                in_=staged_chunks[chunk][:, tiles, :],
+                out=out_view[:, chunk // 2, offset : offset + count, :],
+                in_=staged_chunks[chunk][:, first_tile : first_tile + count, :],
             )
 
         def store_if_full(chunk, j):
             if chunk >= CHUNKS - 2:
-                store(chunk, j, 1)
-            elif (j + 1) % STORE_TILES == 0:
-                store(chunk, j + 1 - STORE_TILES, STORE_TILES)
+                count = 1
+            elif 0 < chunk <= FIRST_CHUNKS:
+                count = TILES
+            else:
+                count = TILES // 2
+            if (j + 1) % count == 0:
+                store(chunk, j + 1 - count, count)
 
         keep_tensor_busy(8)
         for c in range(PASSES):
@@ -246,8 +242,8 @@ def tile_groupedstelinear_t_kernel(tc, x, weight_logits, raw_scales, grad_out, o
             for j in range(TILES):
                 flip(chunk, j)
                 group(chunk, j)
-                if j % 2 == 1:
-                    keep_tensor_busy(2)
+                if chunk == 0 and j % 2 == 1:
+                    keep_tensor_busy(1)
         for c in range(PASSES):
             make_w(0, c)
         quantize_w(0, 0)
@@ -294,9 +290,11 @@ def tile_groupedstelinear_t_kernel(tc, x, weight_logits, raw_scales, grad_out, o
             if ahead < CHUNKS:
                 for j in range(TILES):
                     flip(ahead, j)
-            for j in range(TILES):
-                if ahead < CHUNKS:
+                for j in range(EARLY):
                     group(ahead, j)
+            for j in range(TILES):
+                if ahead < CHUNKS and j + EARLY < TILES:
+                    group(ahead, j + EARLY)
                 multiply(chunk, j, 0, nc.scalar.copy)
                 multiply(chunk, j, 1, nc.vector.tensor_copy)
                 if ahead < CHUNKS:

@@ -129,10 +129,10 @@ def tile_groupedstelinear_t_kernel(tc, x, weight_logits, raw_scales, grad_out, o
             for half in range(HALVES)
         ]
 
-        def make_signs(half, c):
+        def make_signs(half, c, rows):
             nc.vector.tensor_scalar(
-                out=half_sign[half][:, c, :, :].rearrange("p (n i) t -> p n t i", i=PACK),
-                in0=logits[half, c][:].rearrange("p t (n i) -> p n t i", i=PACK),
+                out=half_sign[half][:, c, :, rows].rearrange("p (n i) t -> p n t i", i=PACK),
+                in0=logits[half, c][:, rows, :].rearrange("p t (n i) -> p n t i", i=PACK),
                 scalar1=0.0,
                 scalar2=0.5,
                 op0=ALU.is_ge,
@@ -215,7 +215,7 @@ def tile_groupedstelinear_t_kernel(tc, x, weight_logits, raw_scales, grad_out, o
         def store_if_full(chunk, j):
             if chunk >= CHUNKS - 2:
                 count = 1
-            elif 0 < chunk <= FIRST_CHUNKS:
+            elif 0 < chunk <= FIRST_CHUNKS + 1:
                 count = TILES
             else:
                 count = TILES // 2
@@ -224,7 +224,8 @@ def tile_groupedstelinear_t_kernel(tc, x, weight_logits, raw_scales, grad_out, o
 
         keep_tensor_busy(8)
         for c in range(PASSES):
-            make_signs(0, c)
+            for u in range(2):
+                make_signs(0, c, slice(2 * u, 2 * u + 2))
         softplus = consts.tile([P, PASSES, PACK, GROUPS], F32)
         nc.vector.scalar_tensor_tensor(
             out=softplus[:], in0=raw[:], scalar=0.0, in1=log_term[:], op0=ALU.max, op1=ALU.add
@@ -242,7 +243,7 @@ def tile_groupedstelinear_t_kernel(tc, x, weight_logits, raw_scales, grad_out, o
             for j in range(TILES):
                 flip(chunk, j)
                 group(chunk, j)
-                if chunk == 0 and j % 2 == 1:
+                if 4 * chunk + j in (1, 3, 5):
                     keep_tensor_busy(1)
         for c in range(PASSES):
             make_w(0, c)
@@ -259,11 +260,12 @@ def tile_groupedstelinear_t_kernel(tc, x, weight_logits, raw_scales, grad_out, o
             for j in range(TILES):
                 multiply(chunk, j, 0, nc.scalar.copy)
         for c in range(PASSES):
-            make_signs(1, c)
+            make_signs(1, c, slice(0, PACK))
         make_w(1, 0)
         for chunk in range(HEAD_CHUNKS, FIRST_CHUNKS):
             for j in range(TILES):
                 flip(chunk, j)
+            keep_tensor_busy(2)
             for j in range(TILES):
                 group(chunk, j)
                 quantize_grad(chunk, j)

from contextlib import ExitStack

import concourse.mybir as mybir
from concourse.masks import make_identity

F32 = mybir.dt.float32
BF16 = mybir.dt.bfloat16
U32 = mybir.dt.uint32
U8 = mybir.dt.uint8
E4M3X4 = mybir.dt.float8_e4m3fn_x4
E5M2X4 = mybir.dt.float8_e5m2_x4
ALU = mybir.AluOpType
ACT = mybir.ActivationFunctionType

P = 128
PACK = 4
K_PASS = P * PACK

TOKENS = 4 * 1024
OUT_F = 1024
IN_F = 1024
GROUP = 128
GROUPS = IN_F // GROUP
EPS = 1e-6

PASSES = OUT_F // K_PASS
N_MOVE = 512
HALVES = IN_F // N_MOVE
GROUPS_PER_HALF = N_MOVE // GROUP

TILES = 4
CHUNKS = TOKENS // (TILES * P)
PAIR_TILES = 2 * TILES
PAIRS = CHUNKS // 2

FIRST_CHUNKS = 3
EARLY = 2
HEAD_CHUNKS = 2

FLOPS = 2 * TOKENS * OUT_F * IN_F
BYTES = 2 * TOKENS * OUT_F + 2 * OUT_F * IN_F + 2 * OUT_F * GROUPS + 4 * TOKENS * IN_F


def tile_groupedstelinear_t_kernel(tc, x, weight_logits, raw_scales, grad_out, out):
    nc = tc.nc
    grad_view = grad_out.flatten_outer_dims().rearrange("(b p j) o -> p b j o", p=P, j=PAIR_TILES)
    out_view = out.flatten_outer_dims().rearrange("(b p j) i -> p b j i", p=P, j=PAIR_TILES)

    with ExitStack() as ctx:
        ctx.enter_context(tc.manual_schedule())
        consts = ctx.enter_context(tc.tile_pool(name="consts", bufs=1))
        weights = ctx.enter_context(tc.tile_pool(name="weights", bufs=1))
        grad_pool = ctx.enter_context(tc.tile_pool(name="grad", bufs=PAIRS))
        grouped_pool = ctx.enter_context(tc.tile_pool(name="grouped", bufs=HEAD_CHUNKS * TILES))
        codes_pool = ctx.enter_context(tc.tile_pool(name="codes", bufs=TILES * (FIRST_CHUNKS + 1)))
        staged_pool = ctx.enter_context(tc.tile_pool(name="staged", bufs=4))
        flipped_pool = ctx.enter_context(tc.psum_pool(name="flipped", bufs=4))
        acc_pool = ctx.enter_context(tc.psum_pool(name="acc", bufs=4))

        raw = consts.tile([P, PASSES, PACK, GROUPS], BF16)
        nc.scalar.dma_start(
            out=raw[:].rearrange("p c (u e) g -> p (c u) (e g)", e=2),
            in_=raw_scales.rearrange("(cu p e) g -> p cu (e g)", p=P, e=2),
        )
        logits = {}

        def load_logits(half, c):
            rows = weights.tile([P, PACK, N_MOVE], BF16, name="logits%d%d" % (half, c))
            logits[half, c] = rows
            cols = slice(half * N_MOVE, (half + 1) * N_MOVE)
            for u in range(2):
                first = c * K_PASS + u * 2 * P
                nc.sync.dma_start(
                    out=rows[:, 2 * u : 2 * u + 2, :],
                    in_=weight_logits[first : first + 2 * P, cols].rearrange("(p e) i -> p e i", e=2),
                )

        grad_pairs = []

        def load_grad(pair, tiles_at_once):
            grad = grad_pool.tile([P, PAIR_TILES, OUT_F], BF16)
            grad_pairs.append(grad)
            for first in range(0, PAIR_TILES, tiles_at_once):
                tiles = slice(first, first + tiles_at_once)
                nc.sync.dma_start(out=grad[:, tiles, :], in_=grad_view[:, pair, tiles, :])

        for c in range(PASSES):
            load_logits(0, c)
        load_grad(0, 2)
        for c in range(PASSES):
            load_logits(1, c)
        load_grad(1, TILES)
        for pair in range(2, PAIRS):
            load_grad(pair, PAIR_TILES)

        identity = consts.tile([P, P], F32)
        make_identity(nc, identity[:])
        zeros = consts.tile([P, N_MOVE], BF16)
        nc.vector.memset(zeros[:], 0.0)

        def keep_tensor_busy(count):
            idle = acc_pool.tile([P, N_MOVE], F32, name="acc")
            for step in range(count):
                nc.tensor.matmul(idle[:], lhsT=zeros[:, :P], rhs=zeros[:], start=True, stop=True)

        minus_abs = consts.tile([P, PASSES, PACK, GROUPS], F32)
        nc.vector.scalar_tensor_tensor(
            out=minus_abs[:], in0=raw[:], scalar=-1.0, in1=raw[:], op0=ALU.mult, op1=ALU.min
        )
        decay = consts.tile([P, PASSES, PACK, GROUPS], F32)
        nc.scalar.activation(out=decay[:], in_=minus_abs[:], func=ACT.Exp)
        log_term = consts.tile([P, PASSES, PACK, GROUPS], F32)
        nc.scalar.activation(out=log_term[:], in_=decay[:], func=ACT.Ln, bias=1.0)

        half_sign = [
            weights.tile([P, PASSES, N_MOVE, PACK], BF16, align_bytes=256, name="half_sign%d" % half)
            for half in range(HALVES)
        ]
        w_grouped = [
            weights.tile([P, PASSES, N_MOVE, PACK], BF16, align_bytes=256, name="w_grouped%d" % half)
            for half in range(HALVES)
        ]
        w_codes = [
            weights.tile([P, PASSES, N_MOVE], U32, align_bytes=256, name="w_codes%d" % half)
            for half in range(HALVES)
        ]
        w_scales = [
            weights.tile([P, PASSES, N_MOVE], U8, align_bytes=256, name="w_scales%d" % half)
            for half in range(HALVES)
        ]

        def make_signs(half, c, rows):
            nc.vector.tensor_scalar(
                out=half_sign[half][:, c, :, rows].rearrange("p (n i) t -> p n t i", i=PACK),
                in0=logits[half, c][:, rows, :].rearrange("p t (n i) -> p n t i", i=PACK),
                scalar1=0.0,
                scalar2=0.5,
                op0=ALU.is_ge,
                op1=ALU.subtract,
            )

        def make_w(half, c):
            groups = slice(half * GROUPS_PER_HALF, (half + 1) * GROUPS_PER_HALF)
            nc.vector.tensor_tensor(
                out=w_grouped[half][:, c, :, :].rearrange("p (g i) t -> p g i t", i=GROUP),
                in0=half_sign[half][:, c, :, :].rearrange("p (g i) t -> p g i t", i=GROUP),
                in1=twice_scale[:, c, groups, :].unsqueeze(2).to_broadcast([P, GROUPS_PER_HALF, GROUP, PACK]),
                op=ALU.mult,
            )

        def quantize_w(half, c):
            nc.vector.quantize_mx(
                out=w_codes[half][:, c, :].bitcast(E4M3X4),
                scales=w_scales[half][:, c, :],
                in_=w_grouped[half][:, c, :, :].rearrange("p n t -> p (n t)"),
            )

        flipped_tiles = {}
        grouped_tiles = {}
        grad_codes = {}
        grad_scales = {}

        def flip(chunk, j):
            words = grad_pairs[chunk // 2][:, chunk % 2 * TILES + j, :].bitcast(F32)
            flipped = flipped_pool.tile([P, PASSES * 2, P], F32)
            flipped_tiles[chunk, j] = flipped
            for cu in range(PASSES * 2):
                nc.tensor.transpose(flipped[:, cu, :], words[:, cu * P : (cu + 1) * P], identity[:])

        def group(chunk, j):
            grouped = grouped_pool.tile([P, PASSES * P * PACK], BF16, align_bytes=256)
            grouped_tiles[chunk, j] = grouped
            nc.scalar.copy(
                out=grouped[:].bitcast(F32).rearrange("p (c r u) -> p c r u", c=PASSES, u=2),
                in_=flipped_tiles[chunk, j][:].rearrange("p (c u) r -> p c r u", u=2),
            )

        def quantize_grad(chunk, j):
            codes = codes_pool.tile([P, PASSES, P], U32, align_bytes=256)
            scales = codes_pool.tile([P, PASSES, P], U8, align_bytes=256)
            grad_codes[chunk, j] = codes
            grad_scales[chunk, j] = scales
            nc.vector.quantize_mx(
                out=codes[:].rearrange("p c r -> p (c r)").bitcast(E5M2X4),
                scales=scales[:].rearrange("p c r -> p (c r)"),
                in_=grouped_tiles[chunk, j][:],
            )

        staged_chunks = {}

        def multiply(chunk, j, half, copy_out):
            acc = acc_pool.tile([P, N_MOVE], F32)
            for c in range(PASSES):
                nc.tensor.matmul_mx(
                    out=acc[:],
                    lhsT=grad_codes[chunk, j][:, c, :].bitcast(E5M2X4),
                    lhsT_scale=grad_scales[chunk, j][:, c, :],
                    rhs=w_codes[half][:, c, :].bitcast(E4M3X4),
                    rhs_scale=w_scales[half][:, c, :],
                    start=(c == 0),
                    stop=(c == PASSES - 1),
                )
            if chunk not in staged_chunks:
                staged = staged_pool.tile([P, TILES, IN_F], F32)
                staged_chunks[chunk] = staged
            copy_out(out=staged_chunks[chunk][:, j, half * N_MOVE : (half + 1) * N_MOVE], in_=acc[:])

        def store(chunk, first_tile, count):
            offset = chunk % 2 * TILES + first_tile
            nc.sync.dma_start(
                out=out_view[:, chunk // 2, offset : offset + count, :],
                in_=staged_chunks[chunk][:, first_tile : first_tile + count, :],
            )

        def store_if_full(chunk, j):
            if chunk >= CHUNKS - 2:
                count = 1
            elif 0 < chunk <= FIRST_CHUNKS + 1:
                count = TILES
            else:
                count = TILES // 2
            if (j + 1) % count == 0:
                store(chunk, j + 1 - count, count)

        keep_tensor_busy(8)
        for c in range(PASSES):
            for u in range(2):
                make_signs(0, c, slice(2 * u, 2 * u + 2))
        softplus = consts.tile([P, PASSES, PACK, GROUPS], F32)
        nc.vector.scalar_tensor_tensor(
            out=softplus[:], in0=raw[:], scalar=0.0, in1=log_term[:], op0=ALU.max, op1=ALU.add
        )
        twice_scale = consts.tile([P, PASSES, GROUPS, PACK], BF16)
        nc.vector.tensor_scalar(
            out=twice_scale[:],
            in0=softplus[:].rearrange("p c t g -> p c g t"),
            scalar1=EPS,
            scalar2=2.0,
            op0=ALU.add,
            op1=ALU.mult,
        )
        for chunk in range(HEAD_CHUNKS):
            for j in range(TILES):
                flip(chunk, j)
                group(chunk, j)
                if 4 * chunk + j in (1, 3, 5):
                    keep_tensor_busy(1)
        for c in range(PASSES):
            make_w(0, c)
        quantize_w(0, 0)
        quantize_grad(0, 0)
        quantize_w(0, 1)
        for j in range(1, TILES):
            quantize_grad(0, j)
        for chunk in range(1, HEAD_CHUNKS):
            for j in range(TILES):
                quantize_grad(chunk, j)

        for chunk in range(HEAD_CHUNKS):
            for j in range(TILES):
                multiply(chunk, j, 0, nc.scalar.copy)
        for c in range(PASSES):
            make_signs(1, c, slice(0, PACK))
        make_w(1, 0)
        for chunk in range(HEAD_CHUNKS, FIRST_CHUNKS):
            for j in range(TILES):
                flip(chunk, j)
            keep_tensor_busy(2)
            for j in range(TILES):
                group(chunk, j)
                quantize_grad(chunk, j)
            for j in range(TILES):
                multiply(chunk, j, 0, nc.scalar.copy)
        make_w(1, 1)
        for c in range(PASSES):
            quantize_w(1, c)

        for j in range(TILES):
            flip(FIRST_CHUNKS, j)
        for chunk in range(FIRST_CHUNKS):
            for j in range(TILES):
                ahead, due = divmod(chunk * TILES + j, FIRST_CHUNKS)
                if due == 0:
                    group(FIRST_CHUNKS, ahead)
                multiply(chunk, j, 1, nc.vector.tensor_copy if (chunk * TILES + j) % 2 == 0 else nc.scalar.copy)
                if due == FIRST_CHUNKS - 1:
                    quantize_grad(FIRST_CHUNKS, ahead)
                store_if_full(chunk, j)

        for chunk in range(FIRST_CHUNKS, CHUNKS):
            ahead = chunk + 1
            if ahead < CHUNKS:
                for j in range(TILES):
                    flip(ahead, j)
                for j in range(EARLY):
                    group(ahead, j)
            for j in range(TILES):
                if ahead < CHUNKS and j + EARLY < TILES:
                    group(ahead, j + EARLY)
                multiply(chunk, j, 0, nc.scalar.copy)
                multiply(chunk, j, 1, nc.vector.tensor_copy)
                if ahead < CHUNKS:
                    quantize_grad(ahead, j)
                store_if_full(chunk, j)
